import numpy as np
import ml_dtypes


def mxq(x, axis, fmt="e4m3"):
    dtype, down = {"e4m3": (ml_dtypes.float8_e4m3fn, 7), "e5m2": (ml_dtypes.float8_e5m2, 14)}[fmt]
    v = np.moveaxis(np.asarray(x, np.float32).astype(ml_dtypes.bfloat16).astype(np.float64), axis, -1)
    blocks = v.reshape(v.shape[:-1] + (-1, 32))
    amax = np.abs(blocks).max(-1, keepdims=True)
    byte = np.maximum(np.where(amax > 0, np.frexp(amax)[1] - 1 + 127, 0) - down, 1)
    scale = np.exp2(byte - 127.0)
    codes = (blocks / scale).astype(np.float32).astype(dtype).astype(np.float64)
    return np.moveaxis((codes * scale).reshape(v.shape), -1, axis)


WIDE = False


def mx_kscale(k):
    if not WIDE:
        return np.ones(k)
    levels = np.array([10, -10, 5, -5, 0])
    if k % 512:
        return np.exp2(np.random.permutation(np.resize(levels, k // 32))).repeat(32)
    a = np.empty((k // 512, 16))
    for p in range(k // 512):
        a[p, :8] = np.random.permutation(np.resize(levels, 8))
        for g in range(8):
            far = levels[np.abs(levels - a[p, g]) >= 10]
            a[p, g + 8] = far[np.random.randint(len(far))]
    return np.exp2(a.ravel()).repeat(32)


BF16 = ml_dtypes.bfloat16


def bf(x):
    return np.asarray(x, np.float32).astype(BF16)


def f64(x):
    return np.asarray(x).astype(np.float64)


B, S, D, H, DH = 4, 2048, 1024, 1, 64
ROPE_BASE = 10000.0


def rope_tables():
    inv_freq = 1.0 / (ROPE_BASE ** (f64(np.arange(0, DH, 2)) / DH))
    freqs = f64(np.arange(S))[:, None] * inv_freq[None, :]
    return np.cos(freqs), np.sin(freqs)


def rope_interleaved(t, cos, sin):
    x1 = t[..., 0::2]
    x2 = t[..., 1::2]
    c = cos[None, :, None, :]
    s_ = sin[None, :, None, :]
    even = x1 * c - x2 * s_
    odd = x1 * s_ + x2 * c
    return np.stack((even, odd), axis=-1).reshape(t.shape)


def setup_inputs():
    s = mx_kscale(D)
    return {"x": bf(np.random.standard_normal((B, S, D)) * s),
            "wqk_w": bf(np.random.standard_normal((2 * H * DH, D)) / np.sqrt(D) / s[None, :])}


def reference(x, wqk_w):
    xqk = (mxq(f64(x), 2, "e4m3") @ mxq(f64(wqk_w), 1, "e4m3").T).reshape(B, S, 2, H, DH)
    cos, sin = rope_tables()
    q = rope_interleaved(xqk[:, :, 0], cos, sin).transpose(0, 2, 1, 3)
    k = rope_interleaved(xqk[:, :, 1], cos, sin).transpose(0, 2, 1, 3)
    return q, k

@@ -1,0 +1,269 @@
+import math
+from contextlib import ExitStack
+
+import concourse.mybir as mybir
+from concourse.masks import make_identity
+
+F32 = mybir.dt.float32
+BF16 = mybir.dt.bfloat16
+I32 = mybir.dt.int32
+U32 = mybir.dt.uint32
+U8 = mybir.dt.uint8
+FP8X4 = mybir.dt.float8_e4m3fn_x4
+ALU = mybir.AluOpType
+ACT = mybir.ActivationFunctionType
+
+P = 128
+BATCH, SEQ, D_IN = 4, 2048, 1024
+HEAD = 64
+PAIRS = HEAD // 2
+D_OUT = 2 * HEAD
+ROPE_BASE = 10000.0
+
+K_PASS = 4 * P
+PASSES = D_IN // K_PASS
+WORDS = D_IN // 2
+BANK = 512
+
+POS_PER_PART = SEQ // P
+ROUND_TILES = 4
+ROUNDS_PER_BATCH = POS_PER_PART // ROUND_TILES
+ROUNDS = BATCH * ROUNDS_PER_BATCH
+TILE_SUMS = 2 * D_OUT
+BANK_TILES = BANK // TILE_SUMS
+ROUND_BANKS = ROUND_TILES // BANK_TILES
+LOADS_AHEAD = 10
+FIRST_LOAD_PIECES = ROUND_TILES
+
+ROUND_MAGIC = 1.5 * 2.0**23
+
+FLOPS = 2 * BATCH * SEQ * D_IN * D_OUT
+
+
+def turns_per_position(i):
+    return 1.0 / (ROPE_BASE ** (2.0 * i / HEAD) * 2.0 * math.pi)
+
+
+def tile_attention_pa_t_kernel(tc, x, wqk_w, out_0, out_1):
+    nc = tc.nc
+    with ExitStack() as ctx:
+        const = ctx.enter_context(tc.tile_pool(name="const", bufs=1))
+        row_pool = ctx.enter_context(tc.tile_pool(name="rows", bufs=LOADS_AHEAD + 2))
+        mx_pool = ctx.enter_context(tc.tile_pool(name="mx_operands", bufs=3))
+        rope_pool = ctx.enter_context(tc.tile_pool(name="rope", bufs=2))
+        out_pool = ctx.enter_context(tc.tile_pool(name="rotated", bufs=8))
+        flip_banks = ctx.enter_context(tc.psum_pool(name="flip_banks", bufs=5))
+        sum_banks = ctx.enter_context(tc.psum_pool(name="sum_banks", bufs=3))
+        ctx.enter_context(tc.manual_schedule())
+
+        x_runs = x.rearrange("b (p t) d -> b p (t d)", t=POS_PER_PART)
+        out_runs = [
+            out.rearrange("b h (p t) f -> (b h) p (t f)", t=POS_PER_PART) for out in (out_0, out_1)
+        ]
+
+        def load_round(r, pieces):
+            batch, part = divmod(r, ROUNDS_PER_BATCH)
+            rows = row_pool.tile([P, ROUND_TILES * D_IN], BF16)
+            width = ROUND_TILES * D_IN // pieces
+            for piece in range(pieces):
+                start = (part * pieces + piece) * width
+                nc.sync.dma_start(
+                    out=rows[:, piece * width : (piece + 1) * width],
+                    in_=x_runs[batch, :, start : start + width],
+                )
+            return rows
+
+        def k_onto_partitions(row_words, grouped_words):
+            bank = flip_banks.tile([P, WORDS], F32)
+            for q in range(WORDS // P):
+                g, u = divmod(q, 2)
+                words = row_words[:, 2 * g * P + u : 2 * (g + 1) * P : 2]
+                nc.tensor.transpose(bank[:, q * P : (q + 1) * P], words, identity[:])
+            nc.scalar.copy(
+                out=grouped_words, in_=bank[:].rearrange("p (g u r) -> p g r u", g=PASSES, u=2)
+            )
+
+        position = const.tile([P, POS_PER_PART], I32)
+        nc.gpsimd.iota(
+            position[:], pattern=[[1, POS_PER_PART]], base=0, channel_multiplier=POS_PER_PART
+        )
+        partition = const.tile([P, 1], I32)
+        nc.gpsimd.iota(partition[:], pattern=[[0, 1]], base=0, channel_multiplier=1)
+        identity = const.tile([P, P], F32)
+        make_identity(nc, identity[:])
+
+        rows_of = {0: load_round(0, FIRST_LOAD_PIECES)}
+        w_rows = const.tile([P, D_IN], BF16)
+        nc.sync.dma_start(out=w_rows[:], in_=wqk_w)
+        partner_rows = const.tile([P, D_IN], BF16)
+        w_halves = wqk_w.rearrange("(n e) k -> e n k", e=2)
+        for e in range(2):
+            nc.sync.dma_start(out=partner_rows[e:P:2, :], in_=w_halves[1 - e])
+        for r in range(1, LOADS_AHEAD):
+            rows_of[r] = load_round(r, 1)
+
+        turns = const.tile([P, POS_PER_PART, 2, PAIRS], F32)
+        for i in range(PAIRS):
+            nc.vector.tensor_scalar(
+                out=turns[:, :, 1, i],
+                in0=position[:],
+                scalar1=turns_per_position(i),
+                scalar2=None,
+                op0=ALU.mult,
+            )
+        nc.vector.tensor_scalar(
+            out=turns[:, :, 0, :], in0=turns[:, :, 1, :], scalar1=0.25, scalar2=None, op0=ALU.add
+        )
+        whole_turns = const.tile([P, POS_PER_PART, 2, PAIRS], F32)
+        nc.vector.tensor_scalar(
+            out=whole_turns[:],
+            in0=turns[:],
+            scalar1=ROUND_MAGIC,
+            scalar2=ROUND_MAGIC,
+            op0=ALU.add,
+            op1=ALU.subtract,
+        )
+        part_turns = const.tile([P, POS_PER_PART, 2, PAIRS], F32)
+        nc.vector.tensor_tensor(
+            out=part_turns[:], in0=turns[:], in1=whole_turns[:], op=ALU.subtract
+        )
+
+        w_grouped = const.tile([P, PASSES * TILE_SUMS * 4], BF16, align_bytes=64)
+        w_codes = const.tile([P, PASSES * TILE_SUMS], U32, align_bytes=64)
+        w_scales = const.tile([P, PASSES * TILE_SUMS], U8, align_bytes=64)
+
+        def prepare_weights():
+            odd_partition = const.tile([P, 1], I32)
+            nc.vector.tensor_scalar(
+                out=odd_partition[:], in0=partition[:], scalar1=1, scalar2=None, op0=ALU.bitwise_and
+            )
+            sign = const.tile([P, 1], F32)
+            nc.vector.tensor_scalar(
+                out=sign[:], in0=odd_partition[:], scalar1=2.0, scalar2=-1.0, op0=ALU.mult, op1=ALU.add
+            )
+            nc.vector.tensor_scalar(
+                out=partner_rows[:],
+                in0=partner_rows[:],
+                scalar1=sign[:, 0:1],
+                scalar2=None,
+                op0=ALU.mult,
+            )
+            w_grouped_words = w_grouped[:].bitcast(F32).rearrange(
+                "p (g h r u) -> p h g r u", g=PASSES, h=2, u=2
+            )
+            k_onto_partitions(w_rows[:].bitcast(F32), w_grouped_words[:, 0])
+            k_onto_partitions(partner_rows[:].bitcast(F32), w_grouped_words[:, 1])
+            nc.vector.quantize_mx(
+                out=w_codes[:].bitcast(FP8X4), scales=w_scales[:], in_=w_grouped[:]
+            )
+
+        grouped_of, codes_of, scales_of, sums_of, products_of, rotated_of = {}, {}, {}, {}, {}, {}
+
+        def regroup(r):
+            grouped = mx_pool.tile([P, ROUND_TILES * D_IN], BF16, align_bytes=64)
+            row_words = rows_of[r][:].bitcast(F32)
+            grouped_words = grouped[:].bitcast(F32).rearrange(
+                "p (j g r u) -> p j g r u", j=ROUND_TILES, g=PASSES, u=2
+            )
+            for j in range(ROUND_TILES):
+                k_onto_partitions(row_words[:, j * WORDS : (j + 1) * WORDS], grouped_words[:, j])
+            grouped_of[r] = grouped
+
+        cos_sin = const.tile([P, POS_PER_PART * 2 * PAIRS, 2], F32)
+        ROUND_FACTORS = ROUND_TILES * 2 * PAIRS
+
+        def factors_for_round(n):
+            these = slice(n * ROUND_FACTORS, (n + 1) * ROUND_FACTORS)
+            nc.scalar.activation(
+                out=cos_sin[:, these, :],
+                in_=part_turns[:]
+                .rearrange("p t h i -> p (t h i)")[:, these]
+                .unsqueeze(2)
+                .to_broadcast([P, ROUND_FACTORS, 2]),
+                func=ACT.Sin,
+                scale=2.0 * math.pi,
+            )
+
+        def quantise(r, half):
+            if half == 0:
+                codes = mx_pool.tile([P, ROUND_TILES * PASSES * P], U32, align_bytes=64)
+                scales = mx_pool.tile([P, ROUND_TILES * PASSES * P], U8, align_bytes=64)
+                codes_of[r], scales_of[r] = codes, scales
+            words = BANK_TILES * PASSES * P
+            nc.vector.quantize_mx(
+                out=codes_of[r][:, half * words : (half + 1) * words].bitcast(FP8X4),
+                scales=scales_of[r][:, half * words : (half + 1) * words],
+                in_=grouped_of[r][:, half * 4 * words : (half + 1) * 4 * words],
+            )
+
+        def multiply(r):
+            sums_of[r] = []
+            for first_tile in range(0, ROUND_TILES, BANK_TILES):
+                sums = sum_banks.tile([P, BANK], F32)
+                for j in range(BANK_TILES):
+                    for g in range(PASSES):
+                        at = ((first_tile + j) * PASSES + g) * P
+                        nc.tensor.matmul_mx(
+                            out=sums[:, j * TILE_SUMS : (j + 1) * TILE_SUMS],
+                            lhsT=codes_of[r][:, at : at + P].bitcast(FP8X4),
+                            lhsT_scale=scales_of[r][:, at : at + P],
+                            rhs=w_codes[:, g * TILE_SUMS : (g + 1) * TILE_SUMS].bitcast(FP8X4),
+                            rhs_scale=w_scales[:, g * TILE_SUMS : (g + 1) * TILE_SUMS],
+                            start=(g == 0),
+                            stop=(g == PASSES - 1),
+                        )
+                sums_of[r].append(sums)
+
+        def rotate_half(r, half):
+            if half == 0:
+                products = rope_pool.tile([P, ROUND_TILES * 2, 2, HEAD], F32)
+                rotated = out_pool.tile([P, 2, ROUND_TILES, HEAD], F32)
+                products_of[r], rotated_of[r] = products, rotated
+            bank_rows = BANK_TILES * 2
+            first = (r % ROUNDS_PER_BATCH) * ROUND_TILES * 2 + half * bank_rows
+            factors = cos_sin[:].rearrange("p (th i) e -> p th (i e)", i=PAIRS)
+            nc.vector.tensor_tensor(
+                out=products_of[r][:, half * bank_rows : (half + 1) * bank_rows],
+                in0=sums_of[r][half][:].rearrange("p (th c f) -> p th c f", c=2, f=HEAD),
+                in1=factors[:, first : first + bank_rows]
+                .unsqueeze(2)
+                .to_broadcast([P, bank_rows, 2, HEAD]),
+                op=ALU.mult,
+            )
+            tiles = slice(half * BANK_TILES, (half + 1) * BANK_TILES)
+            by_term = products_of[r][:].rearrange("p (j h) c f -> p h c j f", h=2)
+            nc.gpsimd.tensor_tensor(
+                out=rotated_of[r][:, :, tiles, :],
+                in0=by_term[:, 0, :, tiles, :],
+                in1=by_term[:, 1, :, tiles, :],
+                op=ALU.add,
+            )
+
+        def store(r):
+            batch, part = divmod(r, ROUNDS_PER_BATCH)
+            run = slice(part * ROUND_TILES * HEAD, (part + 1) * ROUND_TILES * HEAD)
+            for c in range(2):
+                nc.sync.dma_start(
+                    out=out_runs[c][batch, :, run],
+                    in_=rotated_of[r][:, c].rearrange("p j f -> p (j f)"),
+                )
+
+        regroup(0)
+        prepare_weights()
+        factors_for_round(0)
+        for s in range(1, ROUNDS + 2):
+            if s + LOADS_AHEAD - 1 < ROUNDS:
+                rows_of[s + LOADS_AHEAD - 1] = load_round(s + LOADS_AHEAD - 1, 1)
+            if s < ROUNDS:
+                regroup(s)
+            if s < ROUNDS_PER_BATCH:
+                factors_for_round(s)
+            for half in range(ROUND_BANKS):
+                if s <= ROUNDS:
+                    quantise(s - 1, half)
+                if s >= 2:
+                    rotate_half(s - 2, half)
+            if s <= ROUNDS:
+                multiply(s - 1)
+            if s >= 2:
+                store(s - 2)

@@ -32,6 +32,7 @@ ROUNDS = BATCH * ROUNDS_PER_BATCH
 TILE_SUMS = 2 * D_OUT
 BANK_TILES = BANK // TILE_SUMS
 ROUND_BANKS = ROUND_TILES // BANK_TILES
+ORDERED_BY = {1: "vector", 2: "scalar", 3: "vector"}
 LOADS_AHEAD = 10
 FIRST_LOAD_PIECES = ROUND_TILES
 
@@ -50,6 +51,7 @@ def tile_attention_pa_t_kernel(tc, x, wqk_w, out_0, out_1):
         const = ctx.enter_context(tc.tile_pool(name="const", bufs=1))
         row_pool = ctx.enter_context(tc.tile_pool(name="rows", bufs=LOADS_AHEAD + 2))
         mx_pool = ctx.enter_context(tc.tile_pool(name="mx_operands", bufs=3))
+        order_pool = ctx.enter_context(tc.tile_pool(name="ordered_words", bufs=2 * len(ORDERED_BY)))
         rope_pool = ctx.enter_context(tc.tile_pool(name="rope", bufs=2))
         out_pool = ctx.enter_context(tc.tile_pool(name="rotated", bufs=8))
         flip_banks = ctx.enter_context(tc.psum_pool(name="flip_banks", bufs=5))
@@ -73,11 +75,23 @@ def tile_attention_pa_t_kernel(tc, x, wqk_w, out_0, out_1):
                 )
             return rows
 
-        def k_onto_partitions(row_words, grouped_words):
+        def put_in_order(rows, engine):
+            ordered = order_pool.tile([P, WORDS], F32)
+            copy = nc.vector.tensor_copy if engine == "vector" else nc.scalar.copy
+            copy(
+                out=ordered[:].rearrange("p (g u w) -> p g u w", g=PASSES, u=2),
+                in_=rows.rearrange("p (g w u) -> p g u w", g=PASSES, u=2),
+            )
+            return ordered
+
+        def k_onto_partitions(row_words, grouped_words, in_order=False):
             bank = flip_banks.tile([P, WORDS], F32)
             for q in range(WORDS // P):
                 g, u = divmod(q, 2)
-                words = row_words[:, 2 * g * P + u : 2 * (g + 1) * P : 2]
+                if in_order:
+                    words = row_words[:, q * P : (q + 1) * P]
+                else:
+                    words = row_words[:, 2 * g * P + u : 2 * (g + 1) * P : 2]
                 nc.tensor.transpose(bank[:, q * P : (q + 1) * P], words, identity[:])
             nc.scalar.copy(
                 out=grouped_words, in_=bank[:].rearrange("p (g u r) -> p g r u", g=PASSES, u=2)
@@ -158,6 +172,12 @@ def tile_attention_pa_t_kernel(tc, x, wqk_w, out_0, out_1):
             )
 
         grouped_of, codes_of, scales_of, sums_of, products_of, rotated_of = {}, {}, {}, {}, {}, {}
+        ordered_of = {}
+
+        def order_tile(r, j):
+            if r in rows_of and j in ORDERED_BY:
+                words = rows_of[r][:].bitcast(F32)[:, j * WORDS : (j + 1) * WORDS]
+                ordered_of[r, j] = put_in_order(words, ORDERED_BY[j])
 
         def regroup(r):
             grouped = mx_pool.tile([P, ROUND_TILES * D_IN], BF16, align_bytes=64)
@@ -166,7 +186,10 @@ def tile_attention_pa_t_kernel(tc, x, wqk_w, out_0, out_1):
                 "p (j g r u) -> p j g r u", j=ROUND_TILES, g=PASSES, u=2
             )
             for j in range(ROUND_TILES):
-                k_onto_partitions(row_words[:, j * WORDS : (j + 1) * WORDS], grouped_words[:, j])
+                if (r, j) in ordered_of:
+                    k_onto_partitions(ordered_of[r, j][:], grouped_words[:, j], in_order=True)
+                else:
+                    k_onto_partitions(row_words[:, j * WORDS : (j + 1) * WORDS], grouped_words[:, j])
             grouped_of[r] = grouped
 
         cos_sin = const.tile([P, POS_PER_PART * 2 * PAIRS, 2], F32)
@@ -254,6 +277,7 @@ def tile_attention_pa_t_kernel(tc, x, wqk_w, out_0, out_1):
         for s in range(1, ROUNDS + 2):
             if s + LOADS_AHEAD - 1 < ROUNDS:
                 rows_of[s + LOADS_AHEAD - 1] = load_round(s + LOADS_AHEAD - 1, 1)
+            order_tile(s + 1, 2)
             if s < ROUNDS:
                 regroup(s)
             if s < ROUNDS_PER_BATCH:
@@ -263,6 +287,7 @@ def tile_attention_pa_t_kernel(tc, x, wqk_w, out_0, out_1):
                     quantise(s - 1, half)
                 if s >= 2:
                     rotate_half(s - 2, half)
+                order_tile(s + 1, 2 * half + 1)
             if s <= ROUNDS:
                 multiply(s - 1)
             if s >= 2:

@@ -179,18 +179,21 @@ def tile_attention_pa_t_kernel(tc, x, wqk_w, out_0, out_1):
                 words = rows_of[r][:].bitcast(F32)[:, j * WORDS : (j + 1) * WORDS]
                 ordered_of[r, j] = put_in_order(words, ORDERED_BY[j])
 
-        def regroup(r):
-            grouped = mx_pool.tile([P, ROUND_TILES * D_IN], BF16, align_bytes=64)
+        def regroup(r, half):
+            if half == 0:
+                grouped_of[r] = mx_pool.tile(
+                    [P, ROUND_TILES * D_IN], BF16, align_bytes=64, name="grouped"
+                )
+            grouped = grouped_of[r]
             row_words = rows_of[r][:].bitcast(F32)
             grouped_words = grouped[:].bitcast(F32).rearrange(
                 "p (j g r u) -> p j g r u", j=ROUND_TILES, g=PASSES, u=2
             )
-            for j in range(ROUND_TILES):
+            for j in range(half * BANK_TILES, (half + 1) * BANK_TILES):
                 if (r, j) in ordered_of:
                     k_onto_partitions(ordered_of[r, j][:], grouped_words[:, j], in_order=True)
                 else:
                     k_onto_partitions(row_words[:, j * WORDS : (j + 1) * WORDS], grouped_words[:, j])
-            grouped_of[r] = grouped
 
         cos_sin = const.tile([P, POS_PER_PART * 2 * PAIRS, 2], F32)
         ROUND_FACTORS = ROUND_TILES * 2 * PAIRS
@@ -219,23 +222,21 @@ def tile_attention_pa_t_kernel(tc, x, wqk_w, out_0, out_1):
                 in_=grouped_of[r][:, half * 4 * words : (half + 1) * 4 * words],
             )
 
-        def multiply(r):
-            sums_of[r] = []
-            for first_tile in range(0, ROUND_TILES, BANK_TILES):
-                sums = sum_banks.tile([P, BANK], F32)
-                for j in range(BANK_TILES):
-                    for g in range(PASSES):
-                        at = ((first_tile + j) * PASSES + g) * P
-                        nc.tensor.matmul_mx(
-                            out=sums[:, j * TILE_SUMS : (j + 1) * TILE_SUMS],
-                            lhsT=codes_of[r][:, at : at + P].bitcast(FP8X4),
-                            lhsT_scale=scales_of[r][:, at : at + P],
-                            rhs=w_codes[:, g * TILE_SUMS : (g + 1) * TILE_SUMS].bitcast(FP8X4),
-                            rhs_scale=w_scales[:, g * TILE_SUMS : (g + 1) * TILE_SUMS],
-                            start=(g == 0),
-                            stop=(g == PASSES - 1),
-                        )
-                sums_of[r].append(sums)
+        def multiply(r, half):
+            sums = sum_banks.tile([P, BANK], F32)
+            for j in range(BANK_TILES):
+                for g in range(PASSES):
+                    at = ((half * BANK_TILES + j) * PASSES + g) * P
+                    nc.tensor.matmul_mx(
+                        out=sums[:, j * TILE_SUMS : (j + 1) * TILE_SUMS],
+                        lhsT=codes_of[r][:, at : at + P].bitcast(FP8X4),
+                        lhsT_scale=scales_of[r][:, at : at + P],
+                        rhs=w_codes[:, g * TILE_SUMS : (g + 1) * TILE_SUMS].bitcast(FP8X4),
+                        rhs_scale=w_scales[:, g * TILE_SUMS : (g + 1) * TILE_SUMS],
+                        start=(g == 0),
+                        stop=(g == PASSES - 1),
+                    )
+            sums_of[r, half] = sums
 
         def rotate_half(r, half):
             if half == 0:
@@ -247,7 +248,7 @@ def tile_attention_pa_t_kernel(tc, x, wqk_w, out_0, out_1):
             factors = cos_sin[:].rearrange("p (th i) e -> p th (i e)", i=PAIRS)
             nc.vector.tensor_tensor(
                 out=products_of[r][:, half * bank_rows : (half + 1) * bank_rows],
-                in0=sums_of[r][half][:].rearrange("p (th c f) -> p th c f", c=2, f=HEAD),
+                in0=sums_of[r, half][:].rearrange("p (th c f) -> p th c f", c=2, f=HEAD),
                 in1=factors[:, first : first + bank_rows]
                 .unsqueeze(2)
                 .to_broadcast([P, bank_rows, 2, HEAD]),
@@ -271,24 +272,25 @@ def tile_attention_pa_t_kernel(tc, x, wqk_w, out_0, out_1):
                     in_=rotated_of[r][:, c].rearrange("p j f -> p (j f)"),
                 )
 
-        regroup(0)
+        for half in range(ROUND_BANKS):
+            regroup(0, half)
         prepare_weights()
         factors_for_round(0)
         for s in range(1, ROUNDS + 2):
             if s + LOADS_AHEAD - 1 < ROUNDS:
                 rows_of[s + LOADS_AHEAD - 1] = load_round(s + LOADS_AHEAD - 1, 1)
             order_tile(s + 1, 2)
-            if s < ROUNDS:
-                regroup(s)
-            if s < ROUNDS_PER_BATCH:
-                factors_for_round(s)
             for half in range(ROUND_BANKS):
+                if s < ROUNDS:
+                    regroup(s, half)
+                if half == 0 and s < ROUNDS_PER_BATCH:
+                    factors_for_round(s)
                 if s <= ROUNDS:
                     quantise(s - 1, half)
                 if s >= 2:
                     rotate_half(s - 2, half)
                 order_tile(s + 1, 2 * half + 1)
-            if s <= ROUNDS:
-                multiply(s - 1)
+                if s <= ROUNDS:
+                    multiply(s - 1, half)
             if s >= 2:
                 store(s - 2)

@@ -33,6 +33,7 @@ TILE_SUMS = 2 * D_OUT
 BANK_TILES = BANK // TILE_SUMS
 ROUND_BANKS = ROUND_TILES // BANK_TILES
 ORDERED_BY = {1: "vector", 2: "scalar", 3: "vector"}
+STORE_AFTER = (3, 7, 11, 13, 14, 15)
 LOADS_AHEAD = 10
 FIRST_LOAD_PIECES = ROUND_TILES
 
@@ -53,7 +54,7 @@ def tile_attention_pa_t_kernel(tc, x, wqk_w, out_0, out_1):
         mx_pool = ctx.enter_context(tc.tile_pool(name="mx_operands", bufs=3))
         order_pool = ctx.enter_context(tc.tile_pool(name="ordered_words", bufs=2 * len(ORDERED_BY)))
         rope_pool = ctx.enter_context(tc.tile_pool(name="rope", bufs=2))
-        out_pool = ctx.enter_context(tc.tile_pool(name="rotated", bufs=8))
+        out_pool = ctx.enter_context(tc.tile_pool(name="rotated", bufs=BATCH))
         flip_banks = ctx.enter_context(tc.psum_pool(name="flip_banks", bufs=5))
         sum_banks = ctx.enter_context(tc.psum_pool(name="sum_banks", bufs=3))
         ctx.enter_context(tc.manual_schedule())
@@ -240,9 +241,9 @@ def tile_attention_pa_t_kernel(tc, x, wqk_w, out_0, out_1):
 
         def rotate_half(r, half):
             if half == 0:
-                products = rope_pool.tile([P, ROUND_TILES * 2, 2, HEAD], F32)
-                rotated = out_pool.tile([P, 2, ROUND_TILES, HEAD], F32)
-                products_of[r], rotated_of[r] = products, rotated
+                products_of[r] = rope_pool.tile(
+                    [P, ROUND_TILES * 2, 2, HEAD], F32, name="products"
+                )
             bank_rows = BANK_TILES * 2
             first = (r % ROUNDS_PER_BATCH) * ROUND_TILES * 2 + half * bank_rows
             factors = cos_sin[:].rearrange("p (th i) e -> p th (i e)", i=PAIRS)
@@ -254,22 +255,33 @@ def tile_attention_pa_t_kernel(tc, x, wqk_w, out_0, out_1):
                 .to_broadcast([P, bank_rows, 2, HEAD]),
                 op=ALU.mult,
             )
+            batch, part = divmod(r, ROUNDS_PER_BATCH)
+            if batch not in rotated_of:
+                rotated_of[batch] = out_pool.tile(
+                    [P, 2, POS_PER_PART, HEAD], F32, name="rotated"
+                )
+            first_tile = part * ROUND_TILES + half * BANK_TILES
             tiles = slice(half * BANK_TILES, (half + 1) * BANK_TILES)
             by_term = products_of[r][:].rearrange("p (j h) c f -> p h c j f", h=2)
             nc.gpsimd.tensor_tensor(
-                out=rotated_of[r][:, :, tiles, :],
+                out=rotated_of[batch][:, :, first_tile : first_tile + BANK_TILES, :],
                 in0=by_term[:, 0, :, tiles, :],
                 in1=by_term[:, 1, :, tiles, :],
                 op=ALU.add,
             )
 
         def store(r):
+            if r not in STORE_AFTER:
+                return
             batch, part = divmod(r, ROUNDS_PER_BATCH)
-            run = slice(part * ROUND_TILES * HEAD, (part + 1) * ROUND_TILES * HEAD)
+            since = max([e + 1 for e in STORE_AFTER if e < r] + [batch * ROUNDS_PER_BATCH])
+            first_tile = (since - batch * ROUNDS_PER_BATCH) * ROUND_TILES
+            tiles = slice(first_tile, (part + 1) * ROUND_TILES)
+            run = slice(first_tile * HEAD, (part + 1) * ROUND_TILES * HEAD)
             for c in range(2):
                 nc.sync.dma_start(
                     out=out_runs[c][batch, :, run],
-                    in_=rotated_of[r][:, c].rearrange("p j f -> p (j f)"),
+                    in_=rotated_of[batch][:, c, tiles].rearrange("p j f -> p (j f)"),
                 )
 
         for half in range(ROUND_BANKS):

@@ -29,10 +29,8 @@ POS_PER_PART = SEQ // P
 ROUND_TILES = 4
 ROUNDS_PER_BATCH = POS_PER_PART // ROUND_TILES
 ROUNDS = BATCH * ROUNDS_PER_BATCH
-TILE_SUMS = 2 * D_OUT
-BANK_TILES = BANK // TILE_SUMS
-ROUND_BANKS = ROUND_TILES // BANK_TILES
-ORDERED_BY = {1: "vector", 2: "scalar", 3: "vector"}
+HALF_TILES = ROUND_TILES // 2
+HALVES = 2
 STORE_AFTER = (3, 7, 11, 13, 14, 15)
 LOADS_AHEAD = 10
 FIRST_LOAD_PIECES = ROUND_TILES
@@ -52,11 +50,10 @@ def tile_attention_pa_t_kernel(tc, x, wqk_w, out_0, out_1):
         const = ctx.enter_context(tc.tile_pool(name="const", bufs=1))
         row_pool = ctx.enter_context(tc.tile_pool(name="rows", bufs=LOADS_AHEAD + 2))
         mx_pool = ctx.enter_context(tc.tile_pool(name="mx_operands", bufs=3))
-        order_pool = ctx.enter_context(tc.tile_pool(name="ordered_words", bufs=2 * len(ORDERED_BY)))
         rope_pool = ctx.enter_context(tc.tile_pool(name="rope", bufs=2))
         out_pool = ctx.enter_context(tc.tile_pool(name="rotated", bufs=BATCH))
-        flip_banks = ctx.enter_context(tc.psum_pool(name="flip_banks", bufs=5))
-        sum_banks = ctx.enter_context(tc.psum_pool(name="sum_banks", bufs=3))
+        flip_banks = ctx.enter_context(tc.psum_pool(name="flip_banks", bufs=6))
+        sum_banks = ctx.enter_context(tc.psum_pool(name="sum_banks", bufs=2))
         ctx.enter_context(tc.manual_schedule())
 
         x_runs = x.rearrange("b (p t) d -> b p (t d)", t=POS_PER_PART)
@@ -76,23 +73,11 @@ def tile_attention_pa_t_kernel(tc, x, wqk_w, out_0, out_1):
                 )
             return rows
 
-        def put_in_order(rows, engine):
-            ordered = order_pool.tile([P, WORDS], F32)
-            copy = nc.vector.tensor_copy if engine == "vector" else nc.scalar.copy
-            copy(
-                out=ordered[:].rearrange("p (g u w) -> p g u w", g=PASSES, u=2),
-                in_=rows.rearrange("p (g w u) -> p g u w", g=PASSES, u=2),
-            )
-            return ordered
-
-        def k_onto_partitions(row_words, grouped_words, in_order=False):
+        def k_onto_partitions(row_words, grouped_words):
             bank = flip_banks.tile([P, WORDS], F32)
             for q in range(WORDS // P):
                 g, u = divmod(q, 2)
-                if in_order:
-                    words = row_words[:, q * P : (q + 1) * P]
-                else:
-                    words = row_words[:, 2 * g * P + u : 2 * (g + 1) * P : 2]
+                words = row_words[:, 2 * g * P + u : 2 * (g + 1) * P : 2]
                 nc.tensor.transpose(bank[:, q * P : (q + 1) * P], words, identity[:])
             nc.scalar.copy(
                 out=grouped_words, in_=bank[:].rearrange("p (g u r) -> p g r u", g=PASSES, u=2)
@@ -102,18 +87,12 @@ def tile_attention_pa_t_kernel(tc, x, wqk_w, out_0, out_1):
         nc.gpsimd.iota(
             position[:], pattern=[[1, POS_PER_PART]], base=0, channel_multiplier=POS_PER_PART
         )
-        partition = const.tile([P, 1], I32)
-        nc.gpsimd.iota(partition[:], pattern=[[0, 1]], base=0, channel_multiplier=1)
         identity = const.tile([P, P], F32)
         make_identity(nc, identity[:])
 
         rows_of = {0: load_round(0, FIRST_LOAD_PIECES)}
         w_rows = const.tile([P, D_IN], BF16)
         nc.sync.dma_start(out=w_rows[:], in_=wqk_w)
-        partner_rows = const.tile([P, D_IN], BF16)
-        w_halves = wqk_w.rearrange("(n e) k -> e n k", e=2)
-        for e in range(2):
-            nc.sync.dma_start(out=partner_rows[e:P:2, :], in_=w_halves[1 - e])
         for r in range(1, LOADS_AHEAD):
             rows_of[r] = load_round(r, 1)
 
@@ -143,130 +122,113 @@ def tile_attention_pa_t_kernel(tc, x, wqk_w, out_0, out_1):
             out=part_turns[:], in0=turns[:], in1=whole_turns[:], op=ALU.subtract
         )
 
-        w_grouped = const.tile([P, PASSES * TILE_SUMS * 4], BF16, align_bytes=64)
-        w_codes = const.tile([P, PASSES * TILE_SUMS], U32, align_bytes=64)
-        w_scales = const.tile([P, PASSES * TILE_SUMS], U8, align_bytes=64)
+        w_grouped = const.tile([P, PASSES * D_OUT * 4], BF16, align_bytes=64)
+        w_codes = const.tile([P, PASSES * D_OUT], U32, align_bytes=64)
+        w_scales = const.tile([P, PASSES * D_OUT], U8, align_bytes=64)
 
         def prepare_weights():
-            odd_partition = const.tile([P, 1], I32)
-            nc.vector.tensor_scalar(
-                out=odd_partition[:], in0=partition[:], scalar1=1, scalar2=None, op0=ALU.bitwise_and
+            k_onto_partitions(
+                w_rows[:].bitcast(F32),
+                w_grouped[:].bitcast(F32).rearrange("p (g r u) -> p g r u", g=PASSES, u=2),
             )
-            sign = const.tile([P, 1], F32)
-            nc.vector.tensor_scalar(
-                out=sign[:], in0=odd_partition[:], scalar1=2.0, scalar2=-1.0, op0=ALU.mult, op1=ALU.add
-            )
-            nc.vector.tensor_scalar(
-                out=partner_rows[:],
-                in0=partner_rows[:],
-                scalar1=sign[:, 0:1],
-                scalar2=None,
-                op0=ALU.mult,
-            )
-            w_grouped_words = w_grouped[:].bitcast(F32).rearrange(
-                "p (g h r u) -> p h g r u", g=PASSES, h=2, u=2
-            )
-            k_onto_partitions(w_rows[:].bitcast(F32), w_grouped_words[:, 0])
-            k_onto_partitions(partner_rows[:].bitcast(F32), w_grouped_words[:, 1])
             nc.vector.quantize_mx(
                 out=w_codes[:].bitcast(FP8X4), scales=w_scales[:], in_=w_grouped[:]
             )
 
         grouped_of, codes_of, scales_of, sums_of, products_of, rotated_of = {}, {}, {}, {}, {}, {}
-        ordered_of = {}
-
-        def order_tile(r, j):
-            if r in rows_of and j in ORDERED_BY:
-                words = rows_of[r][:].bitcast(F32)[:, j * WORDS : (j + 1) * WORDS]
-                ordered_of[r, j] = put_in_order(words, ORDERED_BY[j])
-
-        def regroup(r, half):
-            if half == 0:
-                grouped_of[r] = mx_pool.tile(
-                    [P, ROUND_TILES * D_IN], BF16, align_bytes=64, name="grouped"
-                )
-            grouped = grouped_of[r]
+        def regroup(r):
+            grouped = mx_pool.tile([P, ROUND_TILES * D_IN], BF16, align_bytes=64)
             row_words = rows_of[r][:].bitcast(F32)
             grouped_words = grouped[:].bitcast(F32).rearrange(
                 "p (j g r u) -> p j g r u", j=ROUND_TILES, g=PASSES, u=2
             )
-            for j in range(half * BANK_TILES, (half + 1) * BANK_TILES):
-                if (r, j) in ordered_of:
-                    k_onto_partitions(ordered_of[r, j][:], grouped_words[:, j], in_order=True)
-                else:
-                    k_onto_partitions(row_words[:, j * WORDS : (j + 1) * WORDS], grouped_words[:, j])
+            for j in range(ROUND_TILES):
+                k_onto_partitions(row_words[:, j * WORDS : (j + 1) * WORDS], grouped_words[:, j])
+            grouped_of[r] = grouped
 
-        cos_sin = const.tile([P, POS_PER_PART * 2 * PAIRS, 2], F32)
-        ROUND_FACTORS = ROUND_TILES * 2 * PAIRS
+        factors = const.tile([P, POS_PER_PART, 2, PAIRS, 2], F32)
 
         def factors_for_round(n):
-            these = slice(n * ROUND_FACTORS, (n + 1) * ROUND_FACTORS)
+            these = slice(n * ROUND_TILES, (n + 1) * ROUND_TILES)
             nc.scalar.activation(
-                out=cos_sin[:, these, :],
-                in_=part_turns[:]
-                .rearrange("p t h i -> p (t h i)")[:, these]
-                .unsqueeze(2)
-                .to_broadcast([P, ROUND_FACTORS, 2]),
+                out=factors[:, these, 0],
+                in_=part_turns[:, these, 0]
+                .unsqueeze(3)
+                .to_broadcast([P, ROUND_TILES, PAIRS, 2]),
                 func=ACT.Sin,
                 scale=2.0 * math.pi,
             )
+            for e in range(2):
+                nc.scalar.activation(
+                    out=factors[:, these, 1, :, e],
+                    in_=part_turns[:, these, 1],
+                    func=ACT.Sin,
+                    scale=(2 * e - 1) * 2.0 * math.pi,
+                )
 
         def quantise(r, half):
             if half == 0:
                 codes = mx_pool.tile([P, ROUND_TILES * PASSES * P], U32, align_bytes=64)
                 scales = mx_pool.tile([P, ROUND_TILES * PASSES * P], U8, align_bytes=64)
                 codes_of[r], scales_of[r] = codes, scales
-            words = BANK_TILES * PASSES * P
+            words = HALF_TILES * PASSES * P
             nc.vector.quantize_mx(
                 out=codes_of[r][:, half * words : (half + 1) * words].bitcast(FP8X4),
                 scales=scales_of[r][:, half * words : (half + 1) * words],
                 in_=grouped_of[r][:, half * 4 * words : (half + 1) * 4 * words],
             )
 
-        def multiply(r, half):
+        def multiply(r):
             sums = sum_banks.tile([P, BANK], F32)
-            for j in range(BANK_TILES):
+            for j in range(ROUND_TILES):
                 for g in range(PASSES):
-                    at = ((half * BANK_TILES + j) * PASSES + g) * P
+                    at = (j * PASSES + g) * P
                     nc.tensor.matmul_mx(
-                        out=sums[:, j * TILE_SUMS : (j + 1) * TILE_SUMS],
+                        out=sums[:, j * D_OUT : (j + 1) * D_OUT],
                         lhsT=codes_of[r][:, at : at + P].bitcast(FP8X4),
                         lhsT_scale=scales_of[r][:, at : at + P],
-                        rhs=w_codes[:, g * TILE_SUMS : (g + 1) * TILE_SUMS].bitcast(FP8X4),
-                        rhs_scale=w_scales[:, g * TILE_SUMS : (g + 1) * TILE_SUMS],
+                        rhs=w_codes[:, g * D_OUT : (g + 1) * D_OUT].bitcast(FP8X4),
+                        rhs_scale=w_scales[:, g * D_OUT : (g + 1) * D_OUT],
                         start=(g == 0),
                         stop=(g == PASSES - 1),
                     )
-            sums_of[r, half] = sums
+            sums_of[r] = sums
 
-        def rotate_half(r, half):
-            if half == 0:
-                products_of[r] = rope_pool.tile(
-                    [P, ROUND_TILES * 2, 2, HEAD], F32, name="products"
+        def make_products(r, h):
+            product = rope_pool.tile([P, 2, ROUND_TILES, HEAD], F32, name=("cos_terms", "sin_terms")[h])
+            products_of[r, h] = product
+            first = (r % ROUNDS_PER_BATCH) * ROUND_TILES
+            t = sums_of[r][:].rearrange("p (j c i e) -> p j c i e", c=2, i=PAIRS, e=2)
+            table = factors[:, first : first + ROUND_TILES, h].unsqueeze(2)
+            if h == 0:
+                nc.vector.tensor_tensor(
+                    out=product[:].rearrange("p c j f -> p j c f"),
+                    in0=t.rearrange("p j c i e -> p j c (i e)"),
+                    in1=table.rearrange("p j c i e -> p j c (i e)").to_broadcast(
+                        [P, ROUND_TILES, 2, HEAD]
+                    ),
+                    op=ALU.mult,
                 )
-            bank_rows = BANK_TILES * 2
-            first = (r % ROUNDS_PER_BATCH) * ROUND_TILES * 2 + half * bank_rows
-            factors = cos_sin[:].rearrange("p (th i) e -> p th (i e)", i=PAIRS)
-            nc.vector.tensor_tensor(
-                out=products_of[r][:, half * bank_rows : (half + 1) * bank_rows],
-                in0=sums_of[r, half][:].rearrange("p (th c f) -> p th c f", c=2, f=HEAD),
-                in1=factors[:, first : first + bank_rows]
-                .unsqueeze(2)
-                .to_broadcast([P, bank_rows, 2, HEAD]),
-                op=ALU.mult,
-            )
+            else:
+                nc.vector.tensor_tensor(
+                    out=product[:].rearrange("p c j (i e) -> p j c i e", e=2),
+                    in0=t[:, :, :, :, ::-1],
+                    in1=table.to_broadcast([P, ROUND_TILES, 2, PAIRS, 2]),
+                    op=ALU.mult,
+                )
+
+        def add_terms(r, half):
             batch, part = divmod(r, ROUNDS_PER_BATCH)
             if batch not in rotated_of:
                 rotated_of[batch] = out_pool.tile(
                     [P, 2, POS_PER_PART, HEAD], F32, name="rotated"
                 )
-            first_tile = part * ROUND_TILES + half * BANK_TILES
-            tiles = slice(half * BANK_TILES, (half + 1) * BANK_TILES)
-            by_term = products_of[r][:].rearrange("p (j h) c f -> p h c j f", h=2)
+            first_tile = part * ROUND_TILES + half * HALF_TILES
+            tiles = slice(half * HALF_TILES, (half + 1) * HALF_TILES)
             nc.gpsimd.tensor_tensor(
-                out=rotated_of[batch][:, :, first_tile : first_tile + BANK_TILES, :],
-                in0=by_term[:, 0, :, tiles, :],
-                in1=by_term[:, 1, :, tiles, :],
+                out=rotated_of[batch][:, :, first_tile : first_tile + HALF_TILES, :],
+                in0=products_of[r, 0][:, :, tiles, :],
+                in1=products_of[r, 1][:, :, tiles, :],
                 op=ALU.add,
             )
 
@@ -284,25 +246,25 @@ def tile_attention_pa_t_kernel(tc, x, wqk_w, out_0, out_1):
                     in_=rotated_of[batch][:, c, tiles].rearrange("p j f -> p (j f)"),
                 )
 
-        for half in range(ROUND_BANKS):
-            regroup(0, half)
+        regroup(0)
         prepare_weights()
         factors_for_round(0)
         for s in range(1, ROUNDS + 2):
             if s + LOADS_AHEAD - 1 < ROUNDS:
                 rows_of[s + LOADS_AHEAD - 1] = load_round(s + LOADS_AHEAD - 1, 1)
-            order_tile(s + 1, 2)
-            for half in range(ROUND_BANKS):
-                if s < ROUNDS:
-                    regroup(s, half)
-                if half == 0 and s < ROUNDS_PER_BATCH:
-                    factors_for_round(s)
+            if s < ROUNDS:
+                regroup(s)
+            if s < ROUNDS_PER_BATCH:
+                factors_for_round(s)
+            for half in range(HALVES):
                 if s <= ROUNDS:
                     quantise(s - 1, half)
                 if s >= 2:
-                    rotate_half(s - 2, half)
-                order_tile(s + 1, 2 * half + 1)
-                if s <= ROUNDS:
-                    multiply(s - 1, half)
+                    make_products(s - 2, half)
+            if s >= 2:
+                for half in range(HALVES):
+                    add_terms(s - 2, half)
+            if s <= ROUNDS:
+                multiply(s - 1)
             if s >= 2:
                 store(s - 2)

@@ -29,11 +29,13 @@ POS_PER_PART = SEQ // P
 ROUND_TILES = 4
 ROUNDS_PER_BATCH = POS_PER_PART // ROUND_TILES
 ROUNDS = BATCH * ROUNDS_PER_BATCH
-HALF_TILES = ROUND_TILES // 2
-HALVES = 2
-STORE_AFTER = (3, 7, 11, 13, 14, 15)
+CHUNK_TILES = 2
+LAST_UNITS = ((0, 2), (2, 2))
+UNITS = [(r, 0, ROUND_TILES) for r in range(ROUNDS - 1)] + [(ROUNDS - 1, j, n) for j, n in LAST_UNITS]
+STORE_AFTER = [(r, ROUND_TILES) for r in (3, 7, 11, 13, 14)] + [(ROUNDS - 1, j + n) for j, n in LAST_UNITS]
 LOADS_AHEAD = 10
-FIRST_LOAD_PIECES = ROUND_TILES
+BY_TILE = (D_IN,) * ROUND_TILES
+FIRST_BY_PASS = (D_IN // PASSES,) * PASSES + (D_IN,) * (ROUND_TILES - 1)
 
 ROUND_MAGIC = 1.5 * 2.0**23
 
@@ -61,16 +63,16 @@ def tile_attention_pa_t_kernel(tc, x, wqk_w, out_0, out_1):
             out.rearrange("b h (p t) f -> (b h) p (t f)", t=POS_PER_PART) for out in (out_0, out_1)
         ]
 
-        def load_round(r, pieces):
+        def load_round(r, widths=(ROUND_TILES * D_IN,)):
             batch, part = divmod(r, ROUNDS_PER_BATCH)
             rows = row_pool.tile([P, ROUND_TILES * D_IN], BF16)
-            width = ROUND_TILES * D_IN // pieces
-            for piece in range(pieces):
-                start = (part * pieces + piece) * width
+            at = 0
+            for width in widths:
+                start = part * ROUND_TILES * D_IN + at
                 nc.sync.dma_start(
-                    out=rows[:, piece * width : (piece + 1) * width],
-                    in_=x_runs[batch, :, start : start + width],
+                    out=rows[:, at : at + width], in_=x_runs[batch, :, start : start + width]
                 )
+                at += width
             return rows
 
         def k_onto_partitions(row_words, grouped_words):
@@ -90,11 +92,11 @@ def tile_attention_pa_t_kernel(tc, x, wqk_w, out_0, out_1):
         identity = const.tile([P, P], F32)
         make_identity(nc, identity[:])
 
-        rows_of = {0: load_round(0, FIRST_LOAD_PIECES)}
         w_rows = const.tile([P, D_IN], BF16)
         nc.sync.dma_start(out=w_rows[:], in_=wqk_w)
+        rows_of = {0: load_round(0, FIRST_BY_PASS)}
         for r in range(1, LOADS_AHEAD):
-            rows_of[r] = load_round(r, 1)
+            rows_of[r] = load_round(r, BY_TILE if r == 1 else (ROUND_TILES * D_IN,))
 
         turns = const.tile([P, POS_PER_PART, 2, PAIRS], F32)
         for i in range(PAIRS):
@@ -136,15 +138,18 @@ def tile_attention_pa_t_kernel(tc, x, wqk_w, out_0, out_1):
             )
 
         grouped_of, codes_of, scales_of, sums_of, products_of, rotated_of = {}, {}, {}, {}, {}, {}
-        def regroup(r):
+
+        def regroup(unit):
+            r, first, tiles = unit
             grouped = mx_pool.tile([P, ROUND_TILES * D_IN], BF16, align_bytes=64)
             row_words = rows_of[r][:].bitcast(F32)
             grouped_words = grouped[:].bitcast(F32).rearrange(
                 "p (j g r u) -> p j g r u", j=ROUND_TILES, g=PASSES, u=2
             )
-            for j in range(ROUND_TILES):
-                k_onto_partitions(row_words[:, j * WORDS : (j + 1) * WORDS], grouped_words[:, j])
-            grouped_of[r] = grouped
+            for j in range(tiles):
+                words = slice((first + j) * WORDS, (first + j + 1) * WORDS)
+                k_onto_partitions(row_words[:, words], grouped_words[:, j])
+            grouped_of[unit] = grouped
 
         factors = const.tile([P, POS_PER_PART, 2, PAIRS, 2], F32)
 
@@ -166,105 +171,113 @@ def tile_attention_pa_t_kernel(tc, x, wqk_w, out_0, out_1):
                     scale=(2 * e - 1) * 2.0 * math.pi,
                 )
 
-        def quantise(r, half):
-            if half == 0:
+        def quantise(unit, chunk):
+            r, first, tiles = unit
+            if chunk == 0:
                 codes = mx_pool.tile([P, ROUND_TILES * PASSES * P], U32, align_bytes=64)
                 scales = mx_pool.tile([P, ROUND_TILES * PASSES * P], U8, align_bytes=64)
-                codes_of[r], scales_of[r] = codes, scales
-            words = HALF_TILES * PASSES * P
+                codes_of[unit], scales_of[unit] = codes, scales
+            tile_words = PASSES * P
+            start = chunk * CHUNK_TILES * tile_words
+            end = min((chunk + 1) * CHUNK_TILES, tiles) * tile_words
             nc.vector.quantize_mx(
-                out=codes_of[r][:, half * words : (half + 1) * words].bitcast(FP8X4),
-                scales=scales_of[r][:, half * words : (half + 1) * words],
-                in_=grouped_of[r][:, half * 4 * words : (half + 1) * 4 * words],
+                out=codes_of[unit][:, start:end].bitcast(FP8X4),
+                scales=scales_of[unit][:, start:end],
+                in_=grouped_of[unit][:, 4 * start : 4 * end],
             )
 
-        def multiply(r):
+        def multiply(unit):
+            r, first, tiles = unit
             sums = sum_banks.tile([P, BANK], F32)
-            for j in range(ROUND_TILES):
+            for j in range(tiles):
                 for g in range(PASSES):
                     at = (j * PASSES + g) * P
                     nc.tensor.matmul_mx(
                         out=sums[:, j * D_OUT : (j + 1) * D_OUT],
-                        lhsT=codes_of[r][:, at : at + P].bitcast(FP8X4),
-                        lhsT_scale=scales_of[r][:, at : at + P],
+                        lhsT=codes_of[unit][:, at : at + P].bitcast(FP8X4),
+                        lhsT_scale=scales_of[unit][:, at : at + P],
                         rhs=w_codes[:, g * D_OUT : (g + 1) * D_OUT].bitcast(FP8X4),
                         rhs_scale=w_scales[:, g * D_OUT : (g + 1) * D_OUT],
                         start=(g == 0),
                         stop=(g == PASSES - 1),
                     )
-            sums_of[r] = sums
+            sums_of[unit] = sums
 
-        def make_products(r, h):
+        def make_products(unit, h):
+            r, first, tiles = unit
             product = rope_pool.tile([P, 2, ROUND_TILES, HEAD], F32, name=("cos_terms", "sin_terms")[h])
-            products_of[r, h] = product
-            first = (r % ROUNDS_PER_BATCH) * ROUND_TILES
-            t = sums_of[r][:].rearrange("p (j c i e) -> p j c i e", c=2, i=PAIRS, e=2)
-            table = factors[:, first : first + ROUND_TILES, h].unsqueeze(2)
+            products_of[unit, h] = product
+            position = (r % ROUNDS_PER_BATCH) * ROUND_TILES + first
+            t = sums_of[unit][:, : tiles * D_OUT].rearrange("p (j c i e) -> p j c i e", c=2, i=PAIRS, e=2)
+            table = factors[:, position : position + tiles, h].unsqueeze(2)
             if h == 0:
                 nc.vector.tensor_tensor(
-                    out=product[:].rearrange("p c j f -> p j c f"),
+                    out=product[:, :, :tiles].rearrange("p c j f -> p j c f"),
                     in0=t.rearrange("p j c i e -> p j c (i e)"),
-                    in1=table.rearrange("p j c i e -> p j c (i e)").to_broadcast(
-                        [P, ROUND_TILES, 2, HEAD]
-                    ),
+                    in1=table.rearrange("p j c i e -> p j c (i e)").to_broadcast([P, tiles, 2, HEAD]),
                     op=ALU.mult,
                 )
             else:
                 nc.vector.tensor_tensor(
-                    out=product[:].rearrange("p c j (i e) -> p j c i e", e=2),
+                    out=product[:, :, :tiles].rearrange("p c j (i e) -> p j c i e", e=2),
                     in0=t[:, :, :, :, ::-1],
-                    in1=table.to_broadcast([P, ROUND_TILES, 2, PAIRS, 2]),
+                    in1=table.to_broadcast([P, tiles, 2, PAIRS, 2]),
                     op=ALU.mult,
                 )
 
-        def add_terms(r, half):
+        def add_terms(unit):
+            r, first, tiles = unit
             batch, part = divmod(r, ROUNDS_PER_BATCH)
             if batch not in rotated_of:
                 rotated_of[batch] = out_pool.tile(
                     [P, 2, POS_PER_PART, HEAD], F32, name="rotated"
                 )
-            first_tile = part * ROUND_TILES + half * HALF_TILES
-            tiles = slice(half * HALF_TILES, (half + 1) * HALF_TILES)
-            nc.gpsimd.tensor_tensor(
-                out=rotated_of[batch][:, :, first_tile : first_tile + HALF_TILES, :],
-                in0=products_of[r, 0][:, :, tiles, :],
-                in1=products_of[r, 1][:, :, tiles, :],
-                op=ALU.add,
-            )
-
-        def store(r):
-            if r not in STORE_AFTER:
-                return
-            batch, part = divmod(r, ROUNDS_PER_BATCH)
-            since = max([e + 1 for e in STORE_AFTER if e < r] + [batch * ROUNDS_PER_BATCH])
-            first_tile = (since - batch * ROUNDS_PER_BATCH) * ROUND_TILES
-            tiles = slice(first_tile, (part + 1) * ROUND_TILES)
-            run = slice(first_tile * HEAD, (part + 1) * ROUND_TILES * HEAD)
-            for c in range(2):
-                nc.sync.dma_start(
-                    out=out_runs[c][batch, :, run],
-                    in_=rotated_of[batch][:, c, tiles].rearrange("p j f -> p (j f)"),
+            engine = nc.vector if unit == UNITS[-1] else nc.gpsimd
+            for start in range(0, tiles, CHUNK_TILES):
+                end = min(start + CHUNK_TILES, tiles)
+                at = part * ROUND_TILES + first
+                engine.tensor_tensor(
+                    out=rotated_of[batch][:, :, at + start : at + end, :],
+                    in0=products_of[unit, 0][:, :, start:end, :],
+                    in1=products_of[unit, 1][:, :, start:end, :],
+                    op=ALU.add,
                 )
 
-        regroup(0)
+        def store(unit):
+            r, first, tiles = unit
+            if (r, first + tiles) not in STORE_AFTER:
+                return
+            batch, part = divmod(r, ROUNDS_PER_BATCH)
+            end = part * ROUND_TILES + first + tiles
+            start = stored_to.get(batch, 0)
+            stored_to[batch] = end
+            for c in range(2):
+                nc.sync.dma_start(
+                    out=out_runs[c][batch, :, start * HEAD : end * HEAD],
+                    in_=rotated_of[batch][:, c, start:end].rearrange("p j f -> p (j f)"),
+                )
+
+        stored_to = {}
         prepare_weights()
+        regroup(UNITS[0])
         factors_for_round(0)
-        for s in range(1, ROUNDS + 2):
+        for s in range(1, len(UNITS) + 2):
             if s + LOADS_AHEAD - 1 < ROUNDS:
-                rows_of[s + LOADS_AHEAD - 1] = load_round(s + LOADS_AHEAD - 1, 1)
-            if s < ROUNDS:
-                regroup(s)
+                rows_of[s + LOADS_AHEAD - 1] = load_round(s + LOADS_AHEAD - 1)
+            if s < len(UNITS):
+                regroup(UNITS[s])
             if s < ROUNDS_PER_BATCH:
                 factors_for_round(s)
-            for half in range(HALVES):
-                if s <= ROUNDS:
-                    quantise(s - 1, half)
-                if s >= 2:
-                    make_products(s - 2, half)
-            if s >= 2:
-                for half in range(HALVES):
-                    add_terms(s - 2, half)
-            if s <= ROUNDS:
-                multiply(s - 1)
-            if s >= 2:
-                store(s - 2)
+            to_multiply = UNITS[s - 1] if s <= len(UNITS) else None
+            to_rotate = UNITS[s - 2] if s >= 2 else None
+            for step in range(2):
+                if to_multiply and step * CHUNK_TILES < to_multiply[2]:
+                    quantise(to_multiply, step)
+                if to_rotate:
+                    make_products(to_rotate, step)
+            if to_rotate:
+                add_terms(to_rotate)
+            if to_multiply:
+                multiply(to_multiply)
+            if to_rotate:
+                store(to_rotate)

@@ -34,6 +34,7 @@ LAST_UNITS = ((0, 2), (2, 2))
 UNITS = [(r, 0, ROUND_TILES) for r in range(ROUNDS - 1)] + [(ROUNDS - 1, j, n) for j, n in LAST_UNITS]
 STORE_AFTER = [(r, ROUND_TILES) for r in (3, 7, 11, 13, 14)] + [(ROUNDS - 1, j + n) for j, n in LAST_UNITS]
 LOADS_AHEAD = 10
+ROUNDS_BY_TILE = 3
 BY_TILE = (D_IN,) * ROUND_TILES
 FIRST_BY_PASS = (D_IN // PASSES,) * PASSES + (D_IN,) * (ROUND_TILES - 1)
 
@@ -85,6 +86,11 @@ def tile_attention_pa_t_kernel(tc, x, wqk_w, out_0, out_1):
                 out=grouped_words, in_=bank[:].rearrange("p (g u r) -> p g r u", g=PASSES, u=2)
             )
 
+        sign = const.tile([P, 2], F32)
+        for e in range(2):
+            nc.gpsimd.memset(sign[:, e : e + 1], 2.0 * e - 1.0)
+        first_sine = const.tile([P, 2], F32)
+        nc.scalar.activation(out=first_sine[:], in_=sign[:], func=ACT.Sin)
         position = const.tile([P, POS_PER_PART], I32)
         nc.gpsimd.iota(
             position[:], pattern=[[1, POS_PER_PART]], base=0, channel_multiplier=POS_PER_PART
@@ -96,7 +102,7 @@ def tile_attention_pa_t_kernel(tc, x, wqk_w, out_0, out_1):
         nc.sync.dma_start(out=w_rows[:], in_=wqk_w)
         rows_of = {0: load_round(0, FIRST_BY_PASS)}
         for r in range(1, LOADS_AHEAD):
-            rows_of[r] = load_round(r, BY_TILE if r == 1 else (ROUND_TILES * D_IN,))
+            rows_of[r] = load_round(r, BY_TILE if r < ROUNDS_BY_TILE else (ROUND_TILES * D_IN,))
 
         turns = const.tile([P, POS_PER_PART, 2, PAIRS], F32)
         for i in range(PAIRS):
@@ -151,25 +157,29 @@ def tile_attention_pa_t_kernel(tc, x, wqk_w, out_0, out_1):
                 k_onto_partitions(row_words[:, words], grouped_words[:, j])
             grouped_of[unit] = grouped
 
-        factors = const.tile([P, POS_PER_PART, 2, PAIRS, 2], F32)
+        cosine = const.tile([P, POS_PER_PART, 2, PAIRS], F32)
+        sine = const.tile([P, POS_PER_PART, PAIRS], F32)
+        signed_sine = const.tile([P, POS_PER_PART, PAIRS, 2], F32)
 
-        def factors_for_round(n):
-            these = slice(n * ROUND_TILES, (n + 1) * ROUND_TILES)
+        def make_cosine_and_sine():
             nc.scalar.activation(
-                out=factors[:, these, 0],
-                in_=part_turns[:, these, 0]
-                .unsqueeze(3)
-                .to_broadcast([P, ROUND_TILES, PAIRS, 2]),
+                out=cosine[:],
+                in_=part_turns[:, :, 0].unsqueeze(2).to_broadcast([P, POS_PER_PART, 2, PAIRS]),
                 func=ACT.Sin,
                 scale=2.0 * math.pi,
             )
-            for e in range(2):
-                nc.scalar.activation(
-                    out=factors[:, these, 1, :, e],
-                    in_=part_turns[:, these, 1],
-                    func=ACT.Sin,
-                    scale=(2 * e - 1) * 2.0 * math.pi,
-                )
+            nc.scalar.activation(
+                out=sine[:], in_=part_turns[:, :, 1], func=ACT.Sin, scale=2.0 * math.pi
+            )
+
+        def make_signed_sine():
+            shape = [P, POS_PER_PART, PAIRS, 2]
+            nc.vector.tensor_tensor(
+                out=signed_sine[:],
+                in0=sine[:].unsqueeze(3).to_broadcast(shape),
+                in1=sign[:].unsqueeze(1).unsqueeze(1).to_broadcast(shape),
+                op=ALU.mult,
+            )
 
         def quantise(unit, chunk):
             r, first, tiles = unit
@@ -209,21 +219,17 @@ def tile_attention_pa_t_kernel(tc, x, wqk_w, out_0, out_1):
             products_of[unit, h] = product
             position = (r % ROUNDS_PER_BATCH) * ROUND_TILES + first
             t = sums_of[unit][:, : tiles * D_OUT].rearrange("p (j c i e) -> p j c i e", c=2, i=PAIRS, e=2)
-            table = factors[:, position : position + tiles, h].unsqueeze(2)
+            positions = slice(position, position + tiles)
             if h == 0:
-                nc.vector.tensor_tensor(
-                    out=product[:, :, :tiles].rearrange("p c j f -> p j c f"),
-                    in0=t.rearrange("p j c i e -> p j c (i e)"),
-                    in1=table.rearrange("p j c i e -> p j c (i e)").to_broadcast([P, tiles, 2, HEAD]),
-                    op=ALU.mult,
-                )
+                in0, table = t, cosine[:, positions].unsqueeze(4)
             else:
-                nc.vector.tensor_tensor(
-                    out=product[:, :, :tiles].rearrange("p c j (i e) -> p j c i e", e=2),
-                    in0=t[:, :, :, :, ::-1],
-                    in1=table.to_broadcast([P, tiles, 2, PAIRS, 2]),
-                    op=ALU.mult,
-                )
+                in0, table = t[:, :, :, :, ::-1], signed_sine[:, positions].unsqueeze(2)
+            nc.vector.tensor_tensor(
+                out=product[:, :, :tiles].rearrange("p c j (i e) -> p j c i e", e=2),
+                in0=in0,
+                in1=table.to_broadcast([P, tiles, 2, PAIRS, 2]),
+                op=ALU.mult,
+            )
 
         def add_terms(unit):
             r, first, tiles = unit
@@ -260,14 +266,12 @@ def tile_attention_pa_t_kernel(tc, x, wqk_w, out_0, out_1):
         stored_to = {}
         prepare_weights()
         regroup(UNITS[0])
-        factors_for_round(0)
+        make_cosine_and_sine()
         for s in range(1, len(UNITS) + 2):
             if s + LOADS_AHEAD - 1 < ROUNDS:
                 rows_of[s + LOADS_AHEAD - 1] = load_round(s + LOADS_AHEAD - 1)
             if s < len(UNITS):
                 regroup(UNITS[s])
-            if s < ROUNDS_PER_BATCH:
-                factors_for_round(s)
             to_multiply = UNITS[s - 1] if s <= len(UNITS) else None
             to_rotate = UNITS[s - 2] if s >= 2 else None
             for step in range(2):
@@ -275,6 +279,8 @@ def tile_attention_pa_t_kernel(tc, x, wqk_w, out_0, out_1):
                     quantise(to_multiply, step)
                 if to_rotate:
                     make_products(to_rotate, step)
+            if s == 1:
+                make_signed_sine()
             if to_rotate:
                 add_terms(to_rotate)
             if to_multiply:

@@ -30,7 +30,7 @@ ROUND_TILES = 4
 ROUNDS_PER_BATCH = POS_PER_PART // ROUND_TILES
 ROUNDS = BATCH * ROUNDS_PER_BATCH
 CHUNK_TILES = 2
-LAST_UNITS = ((0, 2), (2, 2))
+LAST_UNITS = ((0, 3), (3, 1))
 UNITS = [(r, 0, ROUND_TILES) for r in range(ROUNDS - 1)] + [(ROUNDS - 1, j, n) for j, n in LAST_UNITS]
 STORE_AFTER = [(r, ROUND_TILES) for r in (3, 7, 11, 13, 14)] + [(ROUNDS - 1, j + n) for j, n in LAST_UNITS]
 LOADS_AHEAD = 10
@@ -53,7 +53,8 @@ def tile_attention_pa_t_kernel(tc, x, wqk_w, out_0, out_1):
         const = ctx.enter_context(tc.tile_pool(name="const", bufs=1))
         row_pool = ctx.enter_context(tc.tile_pool(name="rows", bufs=LOADS_AHEAD + 2))
         mx_pool = ctx.enter_context(tc.tile_pool(name="mx_operands", bufs=3))
-        rope_pool = ctx.enter_context(tc.tile_pool(name="rope", bufs=2))
+        order_pool = ctx.enter_context(tc.tile_pool(name="ordered_words", bufs=2))
+        rope_pool = ctx.enter_context(tc.tile_pool(name="rope", bufs=3))
         out_pool = ctx.enter_context(tc.tile_pool(name="rotated", bufs=BATCH))
         flip_banks = ctx.enter_context(tc.psum_pool(name="flip_banks", bufs=6))
         sum_banks = ctx.enter_context(tc.psum_pool(name="sum_banks", bufs=2))
@@ -76,11 +77,25 @@ def tile_attention_pa_t_kernel(tc, x, wqk_w, out_0, out_1):
                 at += width
             return rows
 
-        def k_onto_partitions(row_words, grouped_words):
+        def put_in_order(r):
+            if r < ROUNDS_PER_BATCH or r == ROUNDS - 1:
+                return
+            ordered = order_pool.tile([P, WORDS], F32)
+            words = rows_of[r][:].bitcast(F32)[:, (ROUND_TILES - 1) * WORDS :]
+            nc.scalar.copy(
+                out=ordered[:].rearrange("p (g u w) -> p g u w", g=PASSES, u=2),
+                in_=words.rearrange("p (g w u) -> p g u w", g=PASSES, u=2),
+            )
+            ordered_of[r] = ordered
+
+        def k_onto_partitions(row_words, grouped_words, in_order=False):
             bank = flip_banks.tile([P, WORDS], F32)
             for q in range(WORDS // P):
                 g, u = divmod(q, 2)
-                words = row_words[:, 2 * g * P + u : 2 * (g + 1) * P : 2]
+                if in_order:
+                    words = row_words[:, q * P : (q + 1) * P]
+                else:
+                    words = row_words[:, 2 * g * P + u : 2 * (g + 1) * P : 2]
                 nc.tensor.transpose(bank[:, q * P : (q + 1) * P], words, identity[:])
             nc.scalar.copy(
                 out=grouped_words, in_=bank[:].rearrange("p (g u r) -> p g r u", g=PASSES, u=2)
@@ -144,6 +159,7 @@ def tile_attention_pa_t_kernel(tc, x, wqk_w, out_0, out_1):
             )
 
         grouped_of, codes_of, scales_of, sums_of, products_of, rotated_of = {}, {}, {}, {}, {}, {}
+        ordered_of = {}
 
         def regroup(unit):
             r, first, tiles = unit
@@ -153,8 +169,11 @@ def tile_attention_pa_t_kernel(tc, x, wqk_w, out_0, out_1):
                 "p (j g r u) -> p j g r u", j=ROUND_TILES, g=PASSES, u=2
             )
             for j in range(tiles):
-                words = slice((first + j) * WORDS, (first + j + 1) * WORDS)
-                k_onto_partitions(row_words[:, words], grouped_words[:, j])
+                if r in ordered_of and j == ROUND_TILES - 1:
+                    k_onto_partitions(ordered_of[r][:], grouped_words[:, j], in_order=True)
+                else:
+                    words = slice((first + j) * WORDS, (first + j + 1) * WORDS)
+                    k_onto_partitions(row_words[:, words], grouped_words[:, j])
             grouped_of[unit] = grouped
 
         cosine = const.tile([P, POS_PER_PART, 2, PAIRS], F32)
@@ -238,9 +257,9 @@ def tile_attention_pa_t_kernel(tc, x, wqk_w, out_0, out_1):
                 rotated_of[batch] = out_pool.tile(
                     [P, 2, POS_PER_PART, HEAD], F32, name="rotated"
                 )
-            engine = nc.vector if unit == UNITS[-1] else nc.gpsimd
-            for start in range(0, tiles, CHUNK_TILES):
-                end = min(start + CHUNK_TILES, tiles)
+            engine, chunk = (nc.vector, tiles) if r == ROUNDS - 1 else (nc.gpsimd, CHUNK_TILES)
+            for start in range(0, tiles, chunk):
+                end = start + chunk
                 at = part * ROUND_TILES + first
                 engine.tensor_tensor(
                     out=rotated_of[batch][:, :, at + start : at + end, :],
@@ -272,6 +291,8 @@ def tile_attention_pa_t_kernel(tc, x, wqk_w, out_0, out_1):
                 rows_of[s + LOADS_AHEAD - 1] = load_round(s + LOADS_AHEAD - 1)
             if s < len(UNITS):
                 regroup(UNITS[s])
+                if s + 1 < ROUNDS:
+                    put_in_order(s + 1)
             to_multiply = UNITS[s - 1] if s <= len(UNITS) else None
             to_rotate = UNITS[s - 2] if s >= 2 else None
             for step in range(2):

@@ -33,6 +33,7 @@ CHUNK_TILES = 2
 LAST_UNITS = ((0, 3), (3, 1))
 UNITS = [(r, 0, ROUND_TILES) for r in range(ROUNDS - 1)] + [(ROUNDS - 1, j, n) for j, n in LAST_UNITS]
 STORE_AFTER = [(r, ROUND_TILES) for r in (3, 7, 11, 13, 14)] + [(ROUNDS - 1, j + n) for j, n in LAST_UNITS]
+FIRST_ORDERED = 3
 LOADS_AHEAD = 10
 ROUNDS_BY_TILE = 3
 BY_TILE = (D_IN,) * ROUND_TILES
@@ -78,7 +79,7 @@ def tile_attention_pa_t_kernel(tc, x, wqk_w, out_0, out_1):
             return rows
 
         def put_in_order(r):
-            if r < ROUNDS_PER_BATCH or r == ROUNDS - 1:
+            if r < FIRST_ORDERED or r == ROUNDS - 1:
                 return
             ordered = order_pool.tile([P, WORDS], F32)
             words = rows_of[r][:].bitcast(F32)[:, (ROUND_TILES - 1) * WORDS :]
@@ -88,7 +89,7 @@ def tile_attention_pa_t_kernel(tc, x, wqk_w, out_0, out_1):
             )
             ordered_of[r] = ordered
 
-        def k_onto_partitions(row_words, grouped_words, in_order=False):
+        def k_onto_partitions(row_words, grouped_words, in_order=False, copy=nc.scalar.copy):
             bank = flip_banks.tile([P, WORDS], F32)
             for q in range(WORDS // P):
                 g, u = divmod(q, 2)
@@ -97,7 +98,7 @@ def tile_attention_pa_t_kernel(tc, x, wqk_w, out_0, out_1):
                 else:
                     words = row_words[:, 2 * g * P + u : 2 * (g + 1) * P : 2]
                 nc.tensor.transpose(bank[:, q * P : (q + 1) * P], words, identity[:])
-            nc.scalar.copy(
+            copy(
                 out=grouped_words, in_=bank[:].rearrange("p (g u r) -> p g r u", g=PASSES, u=2)
             )
 
@@ -173,7 +174,8 @@ def tile_attention_pa_t_kernel(tc, x, wqk_w, out_0, out_1):
                     k_onto_partitions(ordered_of[r][:], grouped_words[:, j], in_order=True)
                 else:
                     words = slice((first + j) * WORDS, (first + j + 1) * WORDS)
-                    k_onto_partitions(row_words[:, words], grouped_words[:, j])
+                    copy = nc.vector.tensor_copy if r == 0 and j >= CHUNK_TILES else nc.scalar.copy
+                    k_onto_partitions(row_words[:, words], grouped_words[:, j], copy=copy)
             grouped_of[unit] = grouped
 
         cosine = const.tile([P, POS_PER_PART, 2, PAIRS], F32)
@@ -277,7 +279,8 @@ def tile_attention_pa_t_kernel(tc, x, wqk_w, out_0, out_1):
             start = stored_to.get(batch, 0)
             stored_to[batch] = end
             for c in range(2):
-                nc.sync.dma_start(
+                engine = nc.scalar if unit == UNITS[-1] and c == 1 else nc.sync
+                engine.dma_start(
                     out=out_runs[c][batch, :, start * HEAD : end * HEAD],
                     in_=rotated_of[batch][:, c, start:end].rearrange("p j f -> p (j f)"),
                 )

import math
from contextlib import ExitStack

import concourse.mybir as mybir
from concourse.masks import make_identity

F32 = mybir.dt.float32
BF16 = mybir.dt.bfloat16
I32 = mybir.dt.int32
U32 = mybir.dt.uint32
U8 = mybir.dt.uint8
FP8X4 = mybir.dt.float8_e4m3fn_x4
ALU = mybir.AluOpType
ACT = mybir.ActivationFunctionType

P = 128
BATCH, SEQ, D_IN = 4, 2048, 1024
HEAD = 64
PAIRS = HEAD // 2
D_OUT = 2 * HEAD
ROPE_BASE = 10000.0

K_PASS = 4 * P
PASSES = D_IN // K_PASS
WORDS = D_IN // 2
BANK = 512

POS_PER_PART = SEQ // P
ROUND_TILES = 4
ROUNDS_PER_BATCH = POS_PER_PART // ROUND_TILES
ROUNDS = BATCH * ROUNDS_PER_BATCH
CHUNK_TILES = 2
LAST_UNITS = ((0, 3), (3, 1))
UNITS = [(r, 0, ROUND_TILES) for r in range(ROUNDS - 1)] + [(ROUNDS - 1, j, n) for j, n in LAST_UNITS]
STORE_AFTER = [(r, ROUND_TILES) for r in (3, 7, 11, 13, 14)] + [(ROUNDS - 1, j + n) for j, n in LAST_UNITS]
FIRST_ORDERED = 3
LOADS_AHEAD = 10
ROUNDS_BY_TILE = 3
BY_TILE = (D_IN,) * ROUND_TILES
FIRST_BY_PASS = (D_IN // PASSES,) * PASSES + (D_IN,) * (ROUND_TILES - 1)

ROUND_MAGIC = 1.5 * 2.0**23

FLOPS = 2 * BATCH * SEQ * D_IN * D_OUT


def turns_per_position(i):
    return 1.0 / (ROPE_BASE ** (2.0 * i / HEAD) * 2.0 * math.pi)


def tile_attention_pa_t_kernel(tc, x, wqk_w, out_0, out_1):
    nc = tc.nc
    with ExitStack() as ctx:
        const = ctx.enter_context(tc.tile_pool(name="const", bufs=1))
        row_pool = ctx.enter_context(tc.tile_pool(name="rows", bufs=LOADS_AHEAD + 2))
        mx_pool = ctx.enter_context(tc.tile_pool(name="mx_operands", bufs=3))
        order_pool = ctx.enter_context(tc.tile_pool(name="ordered_words", bufs=2))
        rope_pool = ctx.enter_context(tc.tile_pool(name="rope", bufs=3))
        out_pool = ctx.enter_context(tc.tile_pool(name="rotated", bufs=BATCH))
        flip_banks = ctx.enter_context(tc.psum_pool(name="flip_banks", bufs=6))
        sum_banks = ctx.enter_context(tc.psum_pool(name="sum_banks", bufs=2))
        ctx.enter_context(tc.manual_schedule())

        x_runs = x.rearrange("b (p t) d -> b p (t d)", t=POS_PER_PART)
        out_runs = [
            out.rearrange("b h (p t) f -> (b h) p (t f)", t=POS_PER_PART) for out in (out_0, out_1)
        ]

        def load_round(r, widths=(ROUND_TILES * D_IN,)):
            batch, part = divmod(r, ROUNDS_PER_BATCH)
            rows = row_pool.tile([P, ROUND_TILES * D_IN], BF16)
            at = 0
            for width in widths:
                start = part * ROUND_TILES * D_IN + at
                nc.sync.dma_start(
                    out=rows[:, at : at + width], in_=x_runs[batch, :, start : start + width]
                )
                at += width
            return rows

        def put_in_order(r):
            if r < FIRST_ORDERED or r == ROUNDS - 1:
                return
            ordered = order_pool.tile([P, WORDS], F32)
            words = rows_of[r][:].bitcast(F32)[:, (ROUND_TILES - 1) * WORDS :]
            nc.scalar.copy(
                out=ordered[:].rearrange("p (g u w) -> p g u w", g=PASSES, u=2),
                in_=words.rearrange("p (g w u) -> p g u w", g=PASSES, u=2),
            )
            ordered_of[r] = ordered

        def k_onto_partitions(row_words, grouped_words, in_order=False, copy=nc.scalar.copy):
            bank = flip_banks.tile([P, WORDS], F32)
            for q in range(WORDS // P):
                g, u = divmod(q, 2)
                if in_order:
                    words = row_words[:, q * P : (q + 1) * P]
                else:
                    words = row_words[:, 2 * g * P + u : 2 * (g + 1) * P : 2]
                nc.tensor.transpose(bank[:, q * P : (q + 1) * P], words, identity[:])
            copy(
                out=grouped_words, in_=bank[:].rearrange("p (g u r) -> p g r u", g=PASSES, u=2)
            )

        sign = const.tile([P, 2], F32)
        for e in range(2):
            nc.gpsimd.memset(sign[:, e : e + 1], 2.0 * e - 1.0)
        first_sine = const.tile([P, 2], F32)
        nc.scalar.activation(out=first_sine[:], in_=sign[:], func=ACT.Sin)
        position = const.tile([P, POS_PER_PART], I32)
        nc.gpsimd.iota(
            position[:], pattern=[[1, POS_PER_PART]], base=0, channel_multiplier=POS_PER_PART
        )
        identity = const.tile([P, P], F32)
        make_identity(nc, identity[:])

        w_rows = const.tile([P, D_IN], BF16)
        nc.sync.dma_start(out=w_rows[:], in_=wqk_w)
        rows_of = {0: load_round(0, FIRST_BY_PASS)}
        for r in range(1, LOADS_AHEAD):
            rows_of[r] = load_round(r, BY_TILE if r < ROUNDS_BY_TILE else (ROUND_TILES * D_IN,))

        turns = const.tile([P, POS_PER_PART, 2, PAIRS], F32)
        for i in range(PAIRS):
            nc.vector.tensor_scalar(
                out=turns[:, :, 1, i],
                in0=position[:],
                scalar1=turns_per_position(i),
                scalar2=None,
                op0=ALU.mult,
            )
        nc.vector.tensor_scalar(
            out=turns[:, :, 0, :], in0=turns[:, :, 1, :], scalar1=0.25, scalar2=None, op0=ALU.add
        )
        whole_turns = const.tile([P, POS_PER_PART, 2, PAIRS], F32)
        nc.vector.tensor_scalar(
            out=whole_turns[:],
            in0=turns[:],
            scalar1=ROUND_MAGIC,
            scalar2=ROUND_MAGIC,
            op0=ALU.add,
            op1=ALU.subtract,
        )
        part_turns = const.tile([P, POS_PER_PART, 2, PAIRS], F32)
        nc.vector.tensor_tensor(
            out=part_turns[:], in0=turns[:], in1=whole_turns[:], op=ALU.subtract
        )

        w_grouped = const.tile([P, PASSES * D_OUT * 4], BF16, align_bytes=64)
        w_codes = const.tile([P, PASSES * D_OUT], U32, align_bytes=64)
        w_scales = const.tile([P, PASSES * D_OUT], U8, align_bytes=64)

        def prepare_weights():
            k_onto_partitions(
                w_rows[:].bitcast(F32),
                w_grouped[:].bitcast(F32).rearrange("p (g r u) -> p g r u", g=PASSES, u=2),
            )
            nc.vector.quantize_mx(
                out=w_codes[:].bitcast(FP8X4), scales=w_scales[:], in_=w_grouped[:]
            )

        grouped_of, codes_of, scales_of, sums_of, products_of, rotated_of = {}, {}, {}, {}, {}, {}
        ordered_of = {}

        def regroup(unit):
            r, first, tiles = unit
            grouped = mx_pool.tile([P, ROUND_TILES * D_IN], BF16, align_bytes=64)
            row_words = rows_of[r][:].bitcast(F32)
            grouped_words = grouped[:].bitcast(F32).rearrange(
                "p (j g r u) -> p j g r u", j=ROUND_TILES, g=PASSES, u=2
            )
            for j in range(tiles):
                if r in ordered_of and j == ROUND_TILES - 1:
                    k_onto_partitions(ordered_of[r][:], grouped_words[:, j], in_order=True)
                else:
                    words = slice((first + j) * WORDS, (first + j + 1) * WORDS)
                    copy = nc.vector.tensor_copy if r == 0 and j >= CHUNK_TILES else nc.scalar.copy
                    k_onto_partitions(row_words[:, words], grouped_words[:, j], copy=copy)
            grouped_of[unit] = grouped

        cosine = const.tile([P, POS_PER_PART, 2, PAIRS], F32)
        sine = const.tile([P, POS_PER_PART, PAIRS], F32)
        signed_sine = const.tile([P, POS_PER_PART, PAIRS, 2], F32)

        def make_cosine_and_sine():
            nc.scalar.activation(
                out=cosine[:],
                in_=part_turns[:, :, 0].unsqueeze(2).to_broadcast([P, POS_PER_PART, 2, PAIRS]),
                func=ACT.Sin,
                scale=2.0 * math.pi,
            )
            nc.scalar.activation(
                out=sine[:], in_=part_turns[:, :, 1], func=ACT.Sin, scale=2.0 * math.pi
            )

        def make_signed_sine():
            shape = [P, POS_PER_PART, PAIRS, 2]
            nc.vector.tensor_tensor(
                out=signed_sine[:],
                in0=sine[:].unsqueeze(3).to_broadcast(shape),
                in1=sign[:].unsqueeze(1).unsqueeze(1).to_broadcast(shape),
                op=ALU.mult,
            )

        def quantise(unit, chunk):
            r, first, tiles = unit
            if chunk == 0:
                codes = mx_pool.tile([P, ROUND_TILES * PASSES * P], U32, align_bytes=64)
                scales = mx_pool.tile([P, ROUND_TILES * PASSES * P], U8, align_bytes=64)
                codes_of[unit], scales_of[unit] = codes, scales
            tile_words = PASSES * P
            start = chunk * CHUNK_TILES * tile_words
            end = min((chunk + 1) * CHUNK_TILES, tiles) * tile_words
            nc.vector.quantize_mx(
                out=codes_of[unit][:, start:end].bitcast(FP8X4),
                scales=scales_of[unit][:, start:end],
                in_=grouped_of[unit][:, 4 * start : 4 * end],
            )

        def multiply(unit):
            r, first, tiles = unit
            sums = sum_banks.tile([P, BANK], F32)
            for j in range(tiles):
                for g in range(PASSES):
                    at = (j * PASSES + g) * P
                    nc.tensor.matmul_mx(
                        out=sums[:, j * D_OUT : (j + 1) * D_OUT],
                        lhsT=codes_of[unit][:, at : at + P].bitcast(FP8X4),
                        lhsT_scale=scales_of[unit][:, at : at + P],
                        rhs=w_codes[:, g * D_OUT : (g + 1) * D_OUT].bitcast(FP8X4),
                        rhs_scale=w_scales[:, g * D_OUT : (g + 1) * D_OUT],
                        start=(g == 0),
                        stop=(g == PASSES - 1),
                    )
            sums_of[unit] = sums

        def make_products(unit, h):
            r, first, tiles = unit
            product = rope_pool.tile([P, 2, ROUND_TILES, HEAD], F32, name=("cos_terms", "sin_terms")[h])
            products_of[unit, h] = product
            position = (r % ROUNDS_PER_BATCH) * ROUND_TILES + first
            t = sums_of[unit][:, : tiles * D_OUT].rearrange("p (j c i e) -> p j c i e", c=2, i=PAIRS, e=2)
            positions = slice(position, position + tiles)
            if h == 0:
                in0, table = t, cosine[:, positions].unsqueeze(4)
            else:
                in0, table = t[:, :, :, :, ::-1], signed_sine[:, positions].unsqueeze(2)
            nc.vector.tensor_tensor(
                out=product[:, :, :tiles].rearrange("p c j (i e) -> p j c i e", e=2),
                in0=in0,
                in1=table.to_broadcast([P, tiles, 2, PAIRS, 2]),
                op=ALU.mult,
            )

        def add_terms(unit):
            r, first, tiles = unit
            batch, part = divmod(r, ROUNDS_PER_BATCH)
            if batch not in rotated_of:
                rotated_of[batch] = out_pool.tile(
                    [P, 2, POS_PER_PART, HEAD], F32, name="rotated"
                )
            engine, chunk = (nc.vector, tiles) if r == ROUNDS - 1 else (nc.gpsimd, CHUNK_TILES)
            for start in range(0, tiles, chunk):
                end = start + chunk
                at = part * ROUND_TILES + first
                engine.tensor_tensor(
                    out=rotated_of[batch][:, :, at + start : at + end, :],
                    in0=products_of[unit, 0][:, :, start:end, :],
                    in1=products_of[unit, 1][:, :, start:end, :],
                    op=ALU.add,
                )

        def store(unit):
            r, first, tiles = unit
            if (r, first + tiles) not in STORE_AFTER:
                return
            batch, part = divmod(r, ROUNDS_PER_BATCH)
            end = part * ROUND_TILES + first + tiles
            start = stored_to.get(batch, 0)
            stored_to[batch] = end
            for c in range(2):
                engine = nc.scalar if unit == UNITS[-1] and c == 1 else nc.sync
                engine.dma_start(
                    out=out_runs[c][batch, :, start * HEAD : end * HEAD],
                    in_=rotated_of[batch][:, c, start:end].rearrange("p j f -> p (j f)"),
                )

        stored_to = {}
        prepare_weights()
        regroup(UNITS[0])
        make_cosine_and_sine()
        for s in range(1, len(UNITS) + 2):
            if s + LOADS_AHEAD - 1 < ROUNDS:
                rows_of[s + LOADS_AHEAD - 1] = load_round(s + LOADS_AHEAD - 1)
            if s < len(UNITS):
                regroup(UNITS[s])
                if s + 1 < ROUNDS:
                    put_in_order(s + 1)
            to_multiply = UNITS[s - 1] if s <= len(UNITS) else None
            to_rotate = UNITS[s - 2] if s >= 2 else None
            for step in range(2):
                if to_multiply and step * CHUNK_TILES < to_multiply[2]:
                    quantise(to_multiply, step)
                if to_rotate:
                    make_products(to_rotate, step)
            if s == 1:
                make_signed_sine()
            if to_rotate:
                add_terms(to_rotate)
            if to_multiply:
                multiply(to_multiply)
            if to_rotate:
                store(to_rotate)
